import numpy as np
import ml_dtypes


def mxq(x, axis, fmt="e4m3"):
    dtype, down = {"e4m3": (ml_dtypes.float8_e4m3fn, 7), "e5m2": (ml_dtypes.float8_e5m2, 14)}[fmt]
    v = np.moveaxis(np.asarray(x, np.float32).astype(ml_dtypes.bfloat16).astype(np.float64), axis, -1)
    blocks = v.reshape(v.shape[:-1] + (-1, 32))
    amax = np.abs(blocks).max(-1, keepdims=True)
    byte = np.maximum(np.where(amax > 0, np.frexp(amax)[1] - 1 + 127, 0) - down, 1)
    scale = np.exp2(byte - 127.0)
    codes = (blocks / scale).astype(np.float32).astype(dtype).astype(np.float64)
    return np.moveaxis((codes * scale).reshape(v.shape), -1, axis)


WIDE = False


def mx_kscale(k):
    if not WIDE:
        return np.ones(k)
    levels = np.array([10, -10, 5, -5, 0])
    a = np.random.permutation(np.resize(levels, k // 512 * 4)).reshape(k // 512, 4)
    idx = np.arange(k)
    return np.exp2(a[idx // 512, idx % 128 // 32])


BF16 = ml_dtypes.bfloat16


def bf(x):
    return np.asarray(x, np.float32).astype(BF16)


def f64(x):
    return np.asarray(x).astype(np.float64)


B, HD, F = 4096, 512, 1024
STEP = 0.1


def setup_inputs():
    s = mx_kscale(HD)
    return {"u_old": bf(np.random.standard_normal((B, HD)) * s),
            "v_old": bf(np.random.standard_normal((B, HD)) / s),
            "W1": bf(np.random.standard_normal((F, HD)) * np.sqrt(6.0 / (HD + F)) / s),
            "b1": bf(np.random.standard_normal(F) * 0.5)}


def reference(u_old, v_old, W1, b1):
    w = f64(W1)
    v_mid = np.tanh((mxq(f64(u_old), 1, "e4m3") @ mxq(w, 1, "e4m3").T) + f64(b1))
    v_sig = mxq(v_mid, 1, "e4m3") @ mxq(w, 0, "e4m3")
    return f64(v_old) + STEP * v_sig

@@ -1,0 +1,237 @@
+from contextlib import ExitStack
+
+import concourse.mybir as mybir
+from concourse.masks import make_identity
+
+F32 = mybir.dt.float32
+BF16 = mybir.dt.bfloat16
+U32 = mybir.dt.uint32
+U8 = mybir.dt.uint8
+FP8X4 = mybir.dt.float8_e4m3fn_x4
+TANH = mybir.ActivationFunctionType.Tanh
+MULT = mybir.AluOpType.mult
+ADD = mybir.AluOpType.add
+
+B, HD, F = 4096, 512, 1024
+STEP = 0.1
+FLOPS = 2 * 2 * B * HD * F
+
+P = 128
+PACK = 4
+K_PASS = P * PACK
+CHUNK = 512
+N_CHUNKS = B // CHUNK
+ROW_TILES = CHUNK // P
+F_PASSES = F // K_PASS
+HALVES = 2
+TILES_PER_BANK = 2
+RUN = 4
+
+
+def transpose_rows(nc, bank, row_tiles, identity):
+    for i, rows in enumerate(row_tiles):
+        words = rows.bitcast(F32)
+        for half in range(HALVES):
+            nc.tensor.transpose(bank[:, i, half, :], words[:, half * P : (half + 1) * P], identity)
+
+
+def words_side_by_side(bank):
+    return bank.rearrange("q i half r -> q i r half")
+
+
+def group_four_rows(nc, grouped, rows):
+    nc.vector.tensor_copy(
+        out=grouped.rearrange("p (c i) t -> p c t i", i=RUN),
+        in_=rows.rearrange("p t (c i) -> p c t i", i=RUN),
+    )
+
+
+def quantise(nc, codes, scales, grouped):
+    nc.vector.quantize_mx(out=codes.bitcast(FP8X4), scales=scales, in_=grouped)
+
+
+def tile_invblock_pa_t_kernel(tc, u_old, v_old, W1, b1, out):
+    nc = tc.nc
+    with ExitStack() as ctx:
+        ctx.enter_context(tc.manual_schedule())
+        keep = ctx.enter_context(tc.tile_pool(name="keep", bufs=1))
+        stream = ctx.enter_context(tc.tile_pool(name="stream", bufs=2))
+        psum = ctx.enter_context(tc.psum_pool(name="psum", bufs=2))
+
+        def chunk_view(dram, c):
+            return dram[c * CHUNK : (c + 1) * CHUNK, :].rearrange("(p j) h -> p j h", j=ROW_TILES)
+
+        u_rows = [keep.tile([P, ROW_TILES, HD], BF16, name="u_rows%d" % c) for c in range(N_CHUNKS)]
+        v_rows = [keep.tile([P, ROW_TILES, HD], BF16, name="v_rows%d" % c) for c in range(N_CHUNKS)]
+        w_rows = [keep.tile([P, PACK, HD], BF16, name="w_rows%d" % g) for g in range(F_PASSES)]
+        bias_bf16 = keep.tile([P, F_PASSES, PACK], BF16)
+
+        nc.scalar.dma_start(out=bias_bf16[:], in_=b1.rearrange("(g p t) -> p g t", g=F_PASSES, t=PACK))
+        nc.sync.dma_start(out=u_rows[0][:], in_=chunk_view(u_old, 0))
+        for g in range(F_PASSES):
+            nc.sync.dma_start(
+                out=w_rows[g][:],
+                in_=W1[g * K_PASS : (g + 1) * K_PASS, :].rearrange("(p t) k -> p t k", t=PACK),
+            )
+        for c in range(1, N_CHUNKS):
+            nc.sync.dma_start(out=u_rows[c][:], in_=chunk_view(u_old, c))
+            nc.sync.dma_start(out=v_rows[c - 1][:], in_=chunk_view(v_old, c - 1))
+        nc.sync.dma_start(out=v_rows[N_CHUNKS - 1][:], in_=chunk_view(v_old, N_CHUNKS - 1))
+
+        identity = keep.tile([P, P], F32)
+        make_identity(nc, identity[:])
+        zero_column = keep.tile([P, 1], F32)
+        warm_column = keep.tile([P, 1], F32)
+        nc.vector.memset(zero_column[:], 0.0)
+        nc.scalar.activation(out=warm_column[:], in_=zero_column[:], func=TANH)
+
+        u_quantised = {}
+        hidden_quantised = {}
+        hidden_grouped = {}
+        out_rows = {}
+
+        def transpose_u(c, second_copy):
+            grouped = stream.tile([P, CHUNK * PACK], BF16, name="u_grouped", align_bytes=64)
+            pairs = grouped[:].bitcast(F32).rearrange("q (j r half) -> q j r half", j=ROW_TILES, half=HALVES)
+            banks = []
+            for i in range(ROW_TILES // TILES_PER_BANK):
+                bank = psum.tile([P, TILES_PER_BANK, HALVES, P], F32, name="u_bank", tag="transposed")
+                first = i * TILES_PER_BANK
+                transpose_rows(nc, bank, [u_rows[c][:, first + n, :] for n in range(TILES_PER_BANK)], identity[:])
+                banks.append(bank)
+            nc.scalar.copy(out=pairs[:, 0:TILES_PER_BANK], in_=words_side_by_side(banks[0][:]))
+            second_copy(out=pairs[:, TILES_PER_BANK:ROW_TILES], in_=words_side_by_side(banks[1][:]))
+            return grouped
+
+        def quantise_u(c, grouped):
+            codes = stream.tile([P, CHUNK], U32, name="u_codes", align_bytes=64)
+            scales = stream.tile([P, CHUNK], U8, name="u_scales", align_bytes=64)
+            quantise(nc, codes[:], scales[:], grouped[:])
+            u_quantised[c] = (codes, scales)
+
+        def hidden_layer(c, g):
+            u_codes, u_scales = u_quantised[c]
+            hidden = stream.tile([P, PACK, CHUNK], BF16, name="hidden", bufs=3)
+            for t in range(PACK):
+                units = slice((g * PACK + t) * P, (g * PACK + t + 1) * P)
+                acc = psum.tile([P, CHUNK], F32, name="hidden_acc", tag="hidden_acc", bufs=4)
+                nc.tensor.matmul_mx(
+                    out=acc[:],
+                    lhsT=w1_codes[:, units].bitcast(FP8X4),
+                    lhsT_scale=w1_scales[:, units],
+                    rhs=u_codes[:].bitcast(FP8X4),
+                    rhs_scale=u_scales[:],
+                    start=True,
+                    stop=True,
+                )
+                column = g * PACK + t
+                nc.scalar.activation(
+                    out=hidden[:, t, :], in_=acc[:], func=TANH, bias=bias[:, column : column + 1]
+                )
+            grouped = stream.tile([P, CHUNK, PACK], BF16, name="hidden_grouped", align_bytes=64)
+            group_four_rows(nc, grouped[:], hidden[:])
+            hidden_grouped[(c, g)] = grouped
+
+        def quantise_hidden(c, g):
+            if g == 0:
+                codes = stream.tile([P, F_PASSES, CHUNK], U32, name="hidden_codes", align_bytes=64)
+                scales = stream.tile([P, F_PASSES, CHUNK], U8, name="hidden_scales", align_bytes=64)
+                hidden_quantised[c] = (codes, scales)
+            codes, scales = hidden_quantised[c]
+            grouped = hidden_grouped[(c, g)]
+            quantise(nc, codes[:, g, :], scales[:, g, :], grouped[:].rearrange("p n t -> p (n t)"))
+
+        def output_tile(c, j):
+            if j == 0:
+                out_rows[c] = stream.tile([P, ROW_TILES, HD], F32, name="out_rows", bufs=3)
+            codes, scales = hidden_quantised[c]
+            rows = slice(j * P, (j + 1) * P)
+            acc = psum.tile([P, HD], F32, name="out_acc", tag="out_acc")
+            for g in range(F_PASSES):
+                nc.tensor.matmul_mx(
+                    out=acc[:],
+                    lhsT=codes[:, g, rows].bitcast(FP8X4),
+                    lhsT_scale=scales[:, g, rows],
+                    rhs=w2_codes[:, g, :].bitcast(FP8X4),
+                    rhs_scale=w2_scales[:, g, :],
+                    start=(g == 0),
+                    stop=(g == F_PASSES - 1),
+                )
+            nc.vector.scalar_tensor_tensor(
+                out=out_rows[c][:, j, :], in0=acc[:], scalar=STEP, in1=v_rows[c][:, j, :], op0=MULT, op1=ADD
+            )
+
+        def store_half(c, half):
+            tiles = slice(half * 2, half * 2 + 2)
+            nc.sync.dma_start(out=chunk_view(out, c)[:, tiles, :], in_=out_rows[c][:, tiles, :])
+
+        u_grouped = transpose_u(0, nc.vector.tensor_copy)
+
+        w1_grouped = keep.tile([P, F * PACK], BF16, align_bytes=64)
+        w1_codes = keep.tile([P, F], U32, align_bytes=64)
+        w1_scales = keep.tile([P, F], U8, align_bytes=64)
+        w1_pairs = w1_grouped[:].bitcast(F32).rearrange(
+            "q (f r half) -> q f r half", f=F_PASSES * PACK, half=HALVES
+        )
+        for g in range(F_PASSES):
+            banks = []
+            for i in range(PACK // TILES_PER_BANK):
+                bank = psum.tile([P, TILES_PER_BANK, HALVES, P], F32, name="w_bank", tag="hidden_acc", bufs=4)
+                first = i * TILES_PER_BANK
+                transpose_rows(nc, bank, [w_rows[g][:, first + n, :] for n in range(TILES_PER_BANK)], identity[:])
+                banks.append(bank)
+            first = g * PACK
+            nc.scalar.copy(
+                out=w1_pairs[:, first : first + TILES_PER_BANK], in_=words_side_by_side(banks[0][:])
+            )
+            nc.vector.tensor_copy(
+                out=w1_pairs[:, first + TILES_PER_BANK : first + PACK], in_=words_side_by_side(banks[1][:])
+            )
+            if g == 0:
+                quantise_u(0, u_grouped)
+        bias = keep.tile([P, F_PASSES * PACK], F32)
+        nc.vector.tensor_copy(out=bias[:], in_=bias_bf16[:].rearrange("p g t -> p (g t)"))
+        for g in range(F_PASSES):
+            units = slice(g * K_PASS, (g + 1) * K_PASS)
+            quantise(
+                nc, w1_codes[:, units], w1_scales[:, units], w1_grouped[:, g * K_PASS * PACK : (g + 1) * K_PASS * PACK]
+            )
+
+        w2_grouped = keep.tile([P, F_PASSES, HD, PACK], BF16, align_bytes=64)
+        w2_codes = keep.tile([P, F_PASSES, HD], U32, align_bytes=64)
+        w2_scales = keep.tile([P, F_PASSES, HD], U8, align_bytes=64)
+        for g in range(F_PASSES):
+            group_four_rows(nc, w2_grouped[:, g], w_rows[g][:])
+        quantise(
+            nc,
+            w2_codes[:].rearrange("p g h -> p (g h)"),
+            w2_scales[:].rearrange("p g h -> p (g h)"),
+            w2_grouped[:].rearrange("p g h t -> p (g h t)"),
+        )
+
+        for c in range(N_CHUNKS + 1):
+            now = c < N_CHUNKS
+            ahead = c + 1 < N_CHUNKS
+            behind = c >= 1
+            if now:
+                hidden_layer(c, 0)
+            if ahead:
+                u_grouped = transpose_u(c + 1, nc.scalar.copy)
+            if behind:
+                output_tile(c - 1, 0)
+            if now:
+                quantise_hidden(c, 0)
+            if behind:
+                output_tile(c - 1, 1)
+                store_half(c - 1, 0)
+            if ahead:
+                quantise_u(c + 1, u_grouped)
+            if now:
+                hidden_layer(c, 1)
+            if behind:
+                output_tile(c - 1, 2)
+            if now:
+                quantise_hidden(c, 1)
+            if behind:
+                output_tile(c - 1, 3)
+                store_half(c - 1, 1)

@@ -39,10 +39,16 @@ def words_side_by_side(bank):
     return bank.rearrange("q i half r -> q i r half")
 
 
-def group_four_rows(nc, grouped, rows):
+def group_four_rows_on_vector(nc, grouped, rows):
     nc.vector.tensor_copy(
         out=grouped.rearrange("p (c i) t -> p c t i", i=RUN),
         in_=rows.rearrange("p t (c i) -> p c t i", i=RUN),
+    )
+
+
+def group_four_rows_on_gpsimd(nc, grouped, rows):
+    nc.gpsimd.tensor_scalar(
+        out=grouped, in0=rows.rearrange("p t n -> p n t"), scalar1=1.0, scalar2=0.0, op0=MULT, op1=ADD
     )
 
 
@@ -56,7 +62,7 @@ def tile_invblock_pa_t_kernel(tc, u_old, v_old, W1, b1, out):
         ctx.enter_context(tc.manual_schedule())
         keep = ctx.enter_context(tc.tile_pool(name="keep", bufs=1))
         stream = ctx.enter_context(tc.tile_pool(name="stream", bufs=2))
-        psum = ctx.enter_context(tc.psum_pool(name="psum", bufs=2))
+        psum = ctx.enter_context(tc.psum_pool(name="psum", bufs=4))
 
         def chunk_view(dram, c):
             return dram[c * CHUNK : (c + 1) * CHUNK, :].rearrange("(p j) h -> p j h", j=ROW_TILES)
@@ -85,36 +91,43 @@ def tile_invblock_pa_t_kernel(tc, u_old, v_old, W1, b1, out):
         nc.vector.memset(zero_column[:], 0.0)
         nc.scalar.activation(out=warm_column[:], in_=zero_column[:], func=TANH)
 
+        u_grouped = {}
         u_quantised = {}
-        hidden_quantised = {}
+        hidden = {}
         hidden_grouped = {}
+        hidden_quantised = {}
+        out_acc = {}
         out_rows = {}
+
+        def live(c):
+            return 0 <= c < N_CHUNKS
 
         def transpose_u(c, second_copy):
             grouped = stream.tile([P, CHUNK * PACK], BF16, name="u_grouped", align_bytes=64)
             pairs = grouped[:].bitcast(F32).rearrange("q (j r half) -> q j r half", j=ROW_TILES, half=HALVES)
             banks = []
             for i in range(ROW_TILES // TILES_PER_BANK):
-                bank = psum.tile([P, TILES_PER_BANK, HALVES, P], F32, name="u_bank", tag="transposed")
+                bank = psum.tile([P, TILES_PER_BANK, HALVES, P], F32, name="u_bank", tag="shared")
                 first = i * TILES_PER_BANK
                 transpose_rows(nc, bank, [u_rows[c][:, first + n, :] for n in range(TILES_PER_BANK)], identity[:])
                 banks.append(bank)
             nc.scalar.copy(out=pairs[:, 0:TILES_PER_BANK], in_=words_side_by_side(banks[0][:]))
             second_copy(out=pairs[:, TILES_PER_BANK:ROW_TILES], in_=words_side_by_side(banks[1][:]))
-            return grouped
+            u_grouped[c] = grouped
 
-        def quantise_u(c, grouped):
+        def quantise_u(c):
             codes = stream.tile([P, CHUNK], U32, name="u_codes", align_bytes=64)
             scales = stream.tile([P, CHUNK], U8, name="u_scales", align_bytes=64)
-            quantise(nc, codes[:], scales[:], grouped[:])
+            quantise(nc, codes[:], scales[:], u_grouped[c][:])
             u_quantised[c] = (codes, scales)
 
         def hidden_layer(c, g):
             u_codes, u_scales = u_quantised[c]
-            hidden = stream.tile([P, PACK, CHUNK], BF16, name="hidden", bufs=3)
+            hidden[(c, g)] = stream.tile([P, PACK, CHUNK], BF16, name="hidden", bufs=3)
             for t in range(PACK):
-                units = slice((g * PACK + t) * P, (g * PACK + t + 1) * P)
-                acc = psum.tile([P, CHUNK], F32, name="hidden_acc", tag="hidden_acc", bufs=4)
+                column = g * PACK + t
+                units = slice(column * P, (column + 1) * P)
+                acc = psum.tile([P, CHUNK], F32, name="hidden_acc", tag="hidden_acc")
                 nc.tensor.matmul_mx(
                     out=acc[:],
                     lhsT=w1_codes[:, units].bitcast(FP8X4),
@@ -124,13 +137,13 @@ def tile_invblock_pa_t_kernel(tc, u_old, v_old, W1, b1, out):
                     start=True,
                     stop=True,
                 )
-                column = g * PACK + t
                 nc.scalar.activation(
-                    out=hidden[:, t, :], in_=acc[:], func=TANH, bias=bias[:, column : column + 1]
+                    out=hidden[(c, g)][:, t, :], in_=acc[:], func=TANH, bias=bias[:, column : column + 1]
                 )
-            grouped = stream.tile([P, CHUNK, PACK], BF16, name="hidden_grouped", align_bytes=64)
-            group_four_rows(nc, grouped[:], hidden[:])
-            hidden_grouped[(c, g)] = grouped
+
+        def group_hidden(c, g, group_four_rows):
+            hidden_grouped[(c, g)] = stream.tile([P, CHUNK, PACK], BF16, name="hidden_grouped", align_bytes=64)
+            group_four_rows(nc, hidden_grouped[(c, g)][:], hidden[(c, g)][:])
 
         def quantise_hidden(c, g):
             if g == 0:
@@ -141,15 +154,13 @@ def tile_invblock_pa_t_kernel(tc, u_old, v_old, W1, b1, out):
             grouped = hidden_grouped[(c, g)]
             quantise(nc, codes[:, g, :], scales[:, g, :], grouped[:].rearrange("p n t -> p (n t)"))
 
-        def output_tile(c, j):
-            if j == 0:
-                out_rows[c] = stream.tile([P, ROW_TILES, HD], F32, name="out_rows", bufs=3)
+        def second_matmul(c, j):
             codes, scales = hidden_quantised[c]
             rows = slice(j * P, (j + 1) * P)
-            acc = psum.tile([P, HD], F32, name="out_acc", tag="out_acc")
+            out_acc[(c, j)] = psum.tile([P, HD], F32, name="out_acc", tag="shared")
             for g in range(F_PASSES):
                 nc.tensor.matmul_mx(
-                    out=acc[:],
+                    out=out_acc[(c, j)][:],
                     lhsT=codes[:, g, rows].bitcast(FP8X4),
                     lhsT_scale=scales[:, g, rows],
                     rhs=w2_codes[:, g, :].bitcast(FP8X4),
@@ -157,15 +168,26 @@ def tile_invblock_pa_t_kernel(tc, u_old, v_old, W1, b1, out):
                     start=(g == 0),
                     stop=(g == F_PASSES - 1),
                 )
-            nc.vector.scalar_tensor_tensor(
-                out=out_rows[c][:, j, :], in0=acc[:], scalar=STEP, in1=v_rows[c][:, j, :], op0=MULT, op1=ADD
-            )
 
-        def store_half(c, half):
+        def finish_half(c, half):
+            if half == 0:
+                out_rows[c] = stream.tile([P, ROW_TILES, HD], F32, name="out_rows", bufs=3)
             tiles = slice(half * 2, half * 2 + 2)
+            for j in range(half * 2, half * 2 + 2):
+                nc.vector.scalar_tensor_tensor(
+                    out=out_rows[c][:, j, :],
+                    in0=out_acc[(c, j)][:],
+                    scalar=STEP,
+                    in1=v_rows[c][:, j, :],
+                    op0=MULT,
+                    op1=ADD,
+                )
             nc.sync.dma_start(out=chunk_view(out, c)[:, tiles, :], in_=out_rows[c][:, tiles, :])
 
-        u_grouped = transpose_u(0, nc.vector.tensor_copy)
+        transpose_u(0, nc.vector.tensor_copy)
+        quantise_u(0)
+        bias = keep.tile([P, F_PASSES * PACK], F32)
+        nc.vector.tensor_copy(out=bias[:], in_=bias_bf16[:].rearrange("p g t -> p (g t)"))
 
         w1_grouped = keep.tile([P, F * PACK], BF16, align_bytes=64)
         w1_codes = keep.tile([P, F], U32, align_bytes=64)
@@ -176,7 +198,7 @@ def tile_invblock_pa_t_kernel(tc, u_old, v_old, W1, b1, out):
         for g in range(F_PASSES):
             banks = []
             for i in range(PACK // TILES_PER_BANK):
-                bank = psum.tile([P, TILES_PER_BANK, HALVES, P], F32, name="w_bank", tag="hidden_acc", bufs=4)
+                bank = psum.tile([P, TILES_PER_BANK, HALVES, P], F32, name="w_bank", tag="hidden_acc")
                 first = i * TILES_PER_BANK
                 transpose_rows(nc, bank, [w_rows[g][:, first + n, :] for n in range(TILES_PER_BANK)], identity[:])
                 banks.append(bank)
@@ -187,11 +209,6 @@ def tile_invblock_pa_t_kernel(tc, u_old, v_old, W1, b1, out):
             nc.vector.tensor_copy(
                 out=w1_pairs[:, first + TILES_PER_BANK : first + PACK], in_=words_side_by_side(banks[1][:])
             )
-            if g == 0:
-                quantise_u(0, u_grouped)
-        bias = keep.tile([P, F_PASSES * PACK], F32)
-        nc.vector.tensor_copy(out=bias[:], in_=bias_bf16[:].rearrange("p g t -> p (g t)"))
-        for g in range(F_PASSES):
             units = slice(g * K_PASS, (g + 1) * K_PASS)
             quantise(
                 nc, w1_codes[:, units], w1_scales[:, units], w1_grouped[:, g * K_PASS * PACK : (g + 1) * K_PASS * PACK]
@@ -200,38 +217,37 @@ def tile_invblock_pa_t_kernel(tc, u_old, v_old, W1, b1, out):
         w2_grouped = keep.tile([P, F_PASSES, HD, PACK], BF16, align_bytes=64)
         w2_codes = keep.tile([P, F_PASSES, HD], U32, align_bytes=64)
         w2_scales = keep.tile([P, F_PASSES, HD], U8, align_bytes=64)
-        for g in range(F_PASSES):
-            group_four_rows(nc, w2_grouped[:, g], w_rows[g][:])
-        quantise(
-            nc,
-            w2_codes[:].rearrange("p g h -> p (g h)"),
-            w2_scales[:].rearrange("p g h -> p (g h)"),
-            w2_grouped[:].rearrange("p g h t -> p (g h t)"),
-        )
 
-        for c in range(N_CHUNKS + 1):
-            now = c < N_CHUNKS
-            ahead = c + 1 < N_CHUNKS
-            behind = c >= 1
-            if now:
+        for c in range(N_CHUNKS + 2):
+            if live(c):
                 hidden_layer(c, 0)
-            if ahead:
-                u_grouped = transpose_u(c + 1, nc.scalar.copy)
-            if behind:
-                output_tile(c - 1, 0)
-            if now:
-                quantise_hidden(c, 0)
-            if behind:
-                output_tile(c - 1, 1)
-                store_half(c - 1, 0)
-            if ahead:
-                quantise_u(c + 1, u_grouped)
-            if now:
+            if live(c - 1):
+                group_hidden(c - 1, 1, group_four_rows_on_gpsimd)
+            if c == 0:
+                for g in range(F_PASSES):
+                    group_four_rows_on_vector(nc, w2_grouped[:, g], w_rows[g][:])
+            if live(c - 2):
+                finish_half(c - 2, 0)
+            if live(c + 1):
+                transpose_u(c + 1, nc.scalar.copy)
+            if live(c - 2):
+                finish_half(c - 2, 1)
+            if live(c - 1):
+                quantise_hidden(c - 1, 1)
+            if live(c):
+                group_hidden(c, 0, group_four_rows_on_vector)
                 hidden_layer(c, 1)
-            if behind:
-                output_tile(c - 1, 2)
-            if now:
-                quantise_hidden(c, 1)
-            if behind:
-                output_tile(c - 1, 3)
-                store_half(c - 1, 1)
+            if live(c + 1):
+                quantise_u(c + 1)
+            if live(c):
+                quantise_hidden(c, 0)
+            if c == 0:
+                quantise(
+                    nc,
+                    w2_codes[:].rearrange("p g h -> p (g h)"),
+                    w2_scales[:].rearrange("p g h -> p (g h)"),
+                    w2_grouped[:].rearrange("p g h t -> p (g h t)"),
+                )
+            if live(c - 1):
+                for j in range(ROW_TILES):
+                    second_matmul(c - 1, j)

@@ -48,7 +48,12 @@ def group_four_rows_on_vector(nc, grouped, rows):
 
 def group_four_rows_on_gpsimd(nc, grouped, rows):
     nc.gpsimd.tensor_scalar(
-        out=grouped, in0=rows.rearrange("p t n -> p n t"), scalar1=1.0, scalar2=0.0, op0=MULT, op1=ADD
+        out=grouped.rearrange("p (c i) t -> p c t i", i=RUN),
+        in0=rows.rearrange("p t (c i) -> p c t i", i=RUN),
+        scalar1=1.0,
+        scalar2=0.0,
+        op0=MULT,
+        op1=ADD,
     )
 
 
@@ -75,10 +80,10 @@ def tile_invblock_pa_t_kernel(tc, u_old, v_old, W1, b1, out):
         nc.scalar.dma_start(out=bias_bf16[:], in_=b1.rearrange("(g p t) -> p g t", g=F_PASSES, t=PACK))
         nc.sync.dma_start(out=u_rows[0][:], in_=chunk_view(u_old, 0))
         for g in range(F_PASSES):
-            nc.sync.dma_start(
-                out=w_rows[g][:],
-                in_=W1[g * K_PASS : (g + 1) * K_PASS, :].rearrange("(p t) k -> p t k", t=PACK),
-            )
+            rows_of_pass = W1[g * K_PASS : (g + 1) * K_PASS, :].rearrange("(p t) k -> p t k", t=PACK)
+            for first in range(0, PACK, TILES_PER_BANK):
+                tiles = slice(first, first + TILES_PER_BANK)
+                nc.sync.dma_start(out=w_rows[g][:, tiles, :], in_=rows_of_pass[:, tiles, :])
         for c in range(1, N_CHUNKS):
             nc.sync.dma_start(out=u_rows[c][:], in_=chunk_view(u_old, c))
             nc.sync.dma_start(out=v_rows[c - 1][:], in_=chunk_view(v_old, c - 1))
@@ -169,20 +174,18 @@ def tile_invblock_pa_t_kernel(tc, u_old, v_old, W1, b1, out):
                     stop=(g == F_PASSES - 1),
                 )
 
-        def finish_half(c, half):
-            if half == 0:
+        def finish_tile(c, j):
+            if j == 0:
                 out_rows[c] = stream.tile([P, ROW_TILES, HD], F32, name="out_rows", bufs=3)
-            tiles = slice(half * 2, half * 2 + 2)
-            for j in range(half * 2, half * 2 + 2):
-                nc.vector.scalar_tensor_tensor(
-                    out=out_rows[c][:, j, :],
-                    in0=out_acc[(c, j)][:],
-                    scalar=STEP,
-                    in1=v_rows[c][:, j, :],
-                    op0=MULT,
-                    op1=ADD,
-                )
-            nc.sync.dma_start(out=chunk_view(out, c)[:, tiles, :], in_=out_rows[c][:, tiles, :])
+            nc.vector.scalar_tensor_tensor(
+                out=out_rows[c][:, j, :],
+                in0=out_acc[(c, j)][:],
+                scalar=STEP,
+                in1=v_rows[c][:, j, :],
+                op0=MULT,
+                op1=ADD,
+            )
+            nc.sync.dma_start(out=chunk_view(out, c)[:, j, :], in_=out_rows[c][:, j, :])
 
         transpose_u(0, nc.vector.tensor_copy)
         quantise_u(0)
@@ -195,23 +198,20 @@ def tile_invblock_pa_t_kernel(tc, u_old, v_old, W1, b1, out):
         w1_pairs = w1_grouped[:].bitcast(F32).rearrange(
             "q (f r half) -> q f r half", f=F_PASSES * PACK, half=HALVES
         )
-        for g in range(F_PASSES):
-            banks = []
-            for i in range(PACK // TILES_PER_BANK):
-                bank = psum.tile([P, TILES_PER_BANK, HALVES, P], F32, name="w_bank", tag="hidden_acc")
-                first = i * TILES_PER_BANK
-                transpose_rows(nc, bank, [w_rows[g][:, first + n, :] for n in range(TILES_PER_BANK)], identity[:])
-                banks.append(bank)
-            first = g * PACK
-            nc.scalar.copy(
-                out=w1_pairs[:, first : first + TILES_PER_BANK], in_=words_side_by_side(banks[0][:])
+        for b in range(F_PASSES * PACK // TILES_PER_BANK):
+            first = b * TILES_PER_BANK
+            bank = psum.tile([P, TILES_PER_BANK, HALVES, P], F32, name="w_bank", tag="hidden_acc")
+            transpose_rows(
+                nc, bank, [w_rows[n // PACK][:, n % PACK, :] for n in range(first, first + TILES_PER_BANK)], identity[:]
             )
-            nc.vector.tensor_copy(
-                out=w1_pairs[:, first + TILES_PER_BANK : first + PACK], in_=words_side_by_side(banks[1][:])
-            )
-            units = slice(g * K_PASS, (g + 1) * K_PASS)
+            copy_out = nc.scalar.copy if b % 2 == 0 else nc.vector.tensor_copy
+            copy_out(out=w1_pairs[:, first : first + TILES_PER_BANK], in_=words_side_by_side(bank[:]))
+            units = slice(first * P, (first + TILES_PER_BANK) * P)
             quantise(
-                nc, w1_codes[:, units], w1_scales[:, units], w1_grouped[:, g * K_PASS * PACK : (g + 1) * K_PASS * PACK]
+                nc,
+                w1_codes[:, units],
+                w1_scales[:, units],
+                w1_grouped[:, first * P * PACK : (first + TILES_PER_BANK) * P * PACK],
             )
 
         w2_grouped = keep.tile([P, F_PASSES, HD, PACK], BF16, align_bytes=64)
@@ -227,11 +227,13 @@ def tile_invblock_pa_t_kernel(tc, u_old, v_old, W1, b1, out):
                 for g in range(F_PASSES):
                     group_four_rows_on_vector(nc, w2_grouped[:, g], w_rows[g][:])
             if live(c - 2):
-                finish_half(c - 2, 0)
+                finish_tile(c - 2, 0)
+                finish_tile(c - 2, 1)
             if live(c + 1):
                 transpose_u(c + 1, nc.scalar.copy)
             if live(c - 2):
-                finish_half(c - 2, 1)
+                finish_tile(c - 2, 2)
+                finish_tile(c - 2, 3)
             if live(c - 1):
                 quantise_hidden(c - 1, 1)
             if live(c):

@@ -25,6 +25,7 @@ ROW_TILES = CHUNK // P
 F_PASSES = F // K_PASS
 HALVES = 2
 TILES_PER_BANK = 2
+ALL_ROWS = slice(0, CHUNK)
 RUN = 4
 
 
@@ -146,24 +147,26 @@ def tile_invblock_pa_t_kernel(tc, u_old, v_old, W1, b1, out):
                     out=hidden[(c, g)][:, t, :], in_=acc[:], func=TANH, bias=bias[:, column : column + 1]
                 )
 
-        def group_hidden(c, g, group_four_rows):
-            hidden_grouped[(c, g)] = stream.tile([P, CHUNK, PACK], BF16, name="hidden_grouped", align_bytes=64)
-            group_four_rows(nc, hidden_grouped[(c, g)][:], hidden[(c, g)][:])
+        def group_hidden(c, g, group_four_rows, rows=ALL_ROWS):
+            if (c, g) not in hidden_grouped:
+                hidden_grouped[(c, g)] = stream.tile([P, CHUNK, PACK], BF16, name="hidden_grouped", align_bytes=64)
+            group_four_rows(nc, hidden_grouped[(c, g)][:, rows, :], hidden[(c, g)][:, :, rows])
 
-        def quantise_hidden(c, g):
-            if g == 0:
+        def quantise_hidden(c, g, rows=ALL_ROWS):
+            if c not in hidden_quantised:
                 codes = stream.tile([P, F_PASSES, CHUNK], U32, name="hidden_codes", align_bytes=64)
                 scales = stream.tile([P, F_PASSES, CHUNK], U8, name="hidden_scales", align_bytes=64)
                 hidden_quantised[c] = (codes, scales)
             codes, scales = hidden_quantised[c]
-            grouped = hidden_grouped[(c, g)]
-            quantise(nc, codes[:, g, :], scales[:, g, :], grouped[:].rearrange("p n t -> p (n t)"))
+            grouped = hidden_grouped[(c, g)][:, rows, :]
+            quantise(nc, codes[:, g, rows], scales[:, g, rows], grouped.rearrange("p n t -> p (n t)"))
 
-        def second_matmul(c, j):
+        def second_matmul(c, j, passes=range(F_PASSES)):
             codes, scales = hidden_quantised[c]
             rows = slice(j * P, (j + 1) * P)
-            out_acc[(c, j)] = psum.tile([P, HD], F32, name="out_acc", tag="shared")
-            for g in range(F_PASSES):
+            if (c, j) not in out_acc:
+                out_acc[(c, j)] = psum.tile([P, HD], F32, name="out_acc", tag="shared")
+            for g in passes:
                 nc.tensor.matmul_mx(
                     out=out_acc[(c, j)][:],
                     lhsT=codes[:, g, rows].bitcast(FP8X4),
@@ -218,10 +221,9 @@ def tile_invblock_pa_t_kernel(tc, u_old, v_old, W1, b1, out):
         w2_codes = keep.tile([P, F_PASSES, HD], U32, align_bytes=64)
         w2_scales = keep.tile([P, F_PASSES, HD], U8, align_bytes=64)
 
-        for c in range(N_CHUNKS + 2):
-            if live(c):
-                hidden_layer(c, 0)
-            if live(c - 1):
+        hidden_layer(0, 0)
+        for c in range(N_CHUNKS):
+            if live(c - 2):
                 group_hidden(c - 1, 1, group_four_rows_on_gpsimd)
             if c == 0:
                 for g in range(F_PASSES):
@@ -234,15 +236,15 @@ def tile_invblock_pa_t_kernel(tc, u_old, v_old, W1, b1, out):
             if live(c - 2):
                 finish_tile(c - 2, 2)
                 finish_tile(c - 2, 3)
+            if c == 1:
+                group_hidden(0, 1, group_four_rows_on_vector)
             if live(c - 1):
                 quantise_hidden(c - 1, 1)
-            if live(c):
-                group_hidden(c, 0, group_four_rows_on_vector)
-                hidden_layer(c, 1)
+            group_hidden(c, 0, group_four_rows_on_vector)
+            hidden_layer(c, 1)
             if live(c + 1):
                 quantise_u(c + 1)
-            if live(c):
-                quantise_hidden(c, 0)
+            quantise_hidden(c, 0)
             if c == 0:
                 quantise(
                     nc,
@@ -251,5 +253,24 @@ def tile_invblock_pa_t_kernel(tc, u_old, v_old, W1, b1, out):
                     w2_grouped[:].rearrange("p g h t -> p (g h t)"),
                 )
             if live(c - 1):
-                for j in range(ROW_TILES):
+                for j in range(ROW_TILES - 1):
                     second_matmul(c - 1, j)
+            if live(c + 1):
+                hidden_layer(c + 1, 0)
+            if live(c - 1):
+                second_matmul(c - 1, ROW_TILES - 1)
+
+        last = N_CHUNKS - 1
+        for j in range(ROW_TILES):
+            finish_tile(last - 1, j)
+        for j in range(ROW_TILES):
+            second_matmul(last, j, passes=(0,))
+        halves = [slice(h * CHUNK // 2, (h + 1) * CHUNK // 2) for h in range(2)]
+        for rows in halves:
+            group_hidden(last, 1, group_four_rows_on_vector, rows)
+        for rows in halves:
+            quantise_hidden(last, 1, rows)
+        for j in range(ROW_TILES):
+            second_matmul(last, j, passes=(1,))
+        for j in range(ROW_TILES):
+            finish_tile(last, j)

@@ -58,6 +58,13 @@ def group_four_rows_on_gpsimd(nc, grouped, rows):
     )
 
 
+def group_four_rows_on_scalar(nc, grouped, rows):
+    nc.scalar.copy(
+        out=grouped.rearrange("p (c i) t -> p c t i", i=RUN),
+        in_=rows.rearrange("p t (c i) -> p c t i", i=RUN),
+    )
+
+
 def quantise(nc, codes, scales, grouped):
     nc.vector.quantize_mx(out=codes.bitcast(FP8X4), scales=scales, in_=grouped)
 
@@ -207,8 +214,7 @@ def tile_invblock_pa_t_kernel(tc, u_old, v_old, W1, b1, out):
             transpose_rows(
                 nc, bank, [w_rows[n // PACK][:, n % PACK, :] for n in range(first, first + TILES_PER_BANK)], identity[:]
             )
-            copy_out = nc.scalar.copy if b % 2 == 0 else nc.vector.tensor_copy
-            copy_out(out=w1_pairs[:, first : first + TILES_PER_BANK], in_=words_side_by_side(bank[:]))
+            nc.scalar.copy(out=w1_pairs[:, first : first + TILES_PER_BANK], in_=words_side_by_side(bank[:]))
             units = slice(first * P, (first + TILES_PER_BANK) * P)
             quantise(
                 nc,
@@ -267,7 +273,7 @@ def tile_invblock_pa_t_kernel(tc, u_old, v_old, W1, b1, out):
             second_matmul(last, j, passes=(0,))
         halves = [slice(h * CHUNK // 2, (h + 1) * CHUNK // 2) for h in range(2)]
         for rows in halves:
-            group_hidden(last, 1, group_four_rows_on_vector, rows)
+            group_hidden(last, 1, group_four_rows_on_scalar, rows)
         for rows in halves:
             quantise_hidden(last, 1, rows)
         for j in range(ROW_TILES):

@@ -26,6 +26,7 @@ F_PASSES = F // K_PASS
 HALVES = 2
 TILES_PER_BANK = 2
 ALL_ROWS = slice(0, CHUNK)
+ALL_COLS = slice(0, HD)
 RUN = 4
 
 
@@ -86,7 +87,9 @@ def tile_invblock_pa_t_kernel(tc, u_old, v_old, W1, b1, out):
         bias_bf16 = keep.tile([P, F_PASSES, PACK], BF16)
 
         nc.scalar.dma_start(out=bias_bf16[:], in_=b1.rearrange("(g p t) -> p g t", g=F_PASSES, t=PACK))
-        nc.sync.dma_start(out=u_rows[0][:], in_=chunk_view(u_old, 0))
+        for first in range(0, ROW_TILES, TILES_PER_BANK):
+            tiles = slice(first, first + TILES_PER_BANK)
+            nc.sync.dma_start(out=u_rows[0][:, tiles, :], in_=chunk_view(u_old, 0)[:, tiles, :])
         for g in range(F_PASSES):
             rows_of_pass = W1[g * K_PASS : (g + 1) * K_PASS, :].rearrange("(p t) k -> p t k", t=PACK)
             for first in range(0, PACK, TILES_PER_BANK):
@@ -156,7 +159,15 @@ def tile_invblock_pa_t_kernel(tc, u_old, v_old, W1, b1, out):
 
         def group_hidden(c, g, group_four_rows, rows=ALL_ROWS):
             if (c, g) not in hidden_grouped:
-                hidden_grouped[(c, g)] = stream.tile([P, CHUNK, PACK], BF16, name="hidden_grouped", align_bytes=64)
+                on_gpsimd = group_four_rows is group_four_rows_on_gpsimd
+                hidden_grouped[(c, g)] = stream.tile(
+                    [P, CHUNK, PACK],
+                    BF16,
+                    name="hidden_grouped",
+                    tag="grouped_on_gpsimd" if on_gpsimd else "grouped",
+                    bufs=1 if on_gpsimd else 2,
+                    align_bytes=64,
+                )
             group_four_rows(nc, hidden_grouped[(c, g)][:, rows, :], hidden[(c, g)][:, :, rows])
 
         def quantise_hidden(c, g, rows=ALL_ROWS):
@@ -184,18 +195,18 @@ def tile_invblock_pa_t_kernel(tc, u_old, v_old, W1, b1, out):
                     stop=(g == F_PASSES - 1),
                 )
 
-        def finish_tile(c, j):
-            if j == 0:
+        def finish_tile(c, j, cols=ALL_COLS):
+            if c not in out_rows:
                 out_rows[c] = stream.tile([P, ROW_TILES, HD], F32, name="out_rows", bufs=3)
             nc.vector.scalar_tensor_tensor(
-                out=out_rows[c][:, j, :],
-                in0=out_acc[(c, j)][:],
+                out=out_rows[c][:, j, cols],
+                in0=out_acc[(c, j)][:, cols],
                 scalar=STEP,
-                in1=v_rows[c][:, j, :],
+                in1=v_rows[c][:, j, cols],
                 op0=MULT,
                 op1=ADD,
             )
-            nc.sync.dma_start(out=chunk_view(out, c)[:, j, :], in_=out_rows[c][:, j, :])
+            nc.sync.dma_start(out=chunk_view(out, c)[:, j, cols], in_=out_rows[c][:, j, cols])
 
         transpose_u(0, nc.vector.tensor_copy)
         quantise_u(0)
@@ -246,11 +257,11 @@ def tile_invblock_pa_t_kernel(tc, u_old, v_old, W1, b1, out):
                 group_hidden(0, 1, group_four_rows_on_vector)
             if live(c - 1):
                 quantise_hidden(c - 1, 1)
-            group_hidden(c, 0, group_four_rows_on_vector)
+            group_hidden(c, 0, group_four_rows_on_vector if live(c + 1) else group_four_rows_on_gpsimd)
             hidden_layer(c, 1)
             if live(c + 1):
                 quantise_u(c + 1)
-            quantise_hidden(c, 0)
+                quantise_hidden(c, 0)
             if c == 0:
                 quantise(
                     nc,
@@ -269,14 +280,18 @@ def tile_invblock_pa_t_kernel(tc, u_old, v_old, W1, b1, out):
         last = N_CHUNKS - 1
         for j in range(ROW_TILES):
             finish_tile(last - 1, j)
-        for j in range(ROW_TILES):
-            second_matmul(last, j, passes=(0,))
+        quantise_hidden(last, 0)
         halves = [slice(h * CHUNK // 2, (h + 1) * CHUNK // 2) for h in range(2)]
+        tiles_per_half = ROW_TILES // 2
         for rows in halves:
             group_hidden(last, 1, group_four_rows_on_scalar, rows)
         for rows in halves:
             quantise_hidden(last, 1, rows)
-        for j in range(ROW_TILES):
-            second_matmul(last, j, passes=(1,))
-        for j in range(ROW_TILES):
+        for first in range(0, ROW_TILES, tiles_per_half):
+            for g in range(F_PASSES):
+                for j in range(first, first + tiles_per_half):
+                    second_matmul(last, j, passes=(g,))
+        for j in range(ROW_TILES - 1):
             finish_tile(last, j)
+        for h in range(2):
+            finish_tile(last, ROW_TILES - 1, slice(h * HD // 2, (h + 1) * HD // 2))

@@ -27,6 +27,7 @@ HALVES = 2
 TILES_PER_BANK = 2
 ALL_ROWS = slice(0, CHUNK)
 ALL_COLS = slice(0, HD)
+HEAD_WARMERS = 5
 RUN = 4
 
 
@@ -102,10 +103,22 @@ def tile_invblock_pa_t_kernel(tc, u_old, v_old, W1, b1, out):
 
         identity = keep.tile([P, P], F32)
         make_identity(nc, identity[:])
+        idle_operand = keep.tile([P, CHUNK], BF16)
+        nc.vector.memset(idle_operand[:], 0.0)
         zero_column = keep.tile([P, 1], F32)
         warm_column = keep.tile([P, 1], F32)
         nc.vector.memset(zero_column[:], 0.0)
         nc.scalar.activation(out=warm_column[:], in_=zero_column[:], func=TANH)
+
+        idle_acc = psum.tile([P, CHUNK], F32, name="idle_acc", tag="shared")
+
+        def keep_tensor_clock_up(count):
+            for unused in range(count):
+                nc.tensor.matmul(
+                    idle_acc[:], lhsT=idle_operand[:, 0:P], rhs=idle_operand[:], start=True, stop=True
+                )
+
+        keep_tensor_clock_up(HEAD_WARMERS)
 
         u_grouped = {}
         u_quantised = {}
@@ -209,6 +222,7 @@ def tile_invblock_pa_t_kernel(tc, u_old, v_old, W1, b1, out):
             nc.sync.dma_start(out=chunk_view(out, c)[:, j, cols], in_=out_rows[c][:, j, cols])
 
         transpose_u(0, nc.vector.tensor_copy)
+        keep_tensor_clock_up(1)
         quantise_u(0)
         bias = keep.tile([P, F_PASSES * PACK], F32)
         nc.vector.tensor_copy(out=bias[:], in_=bias_bf16[:].rearrange("p g t -> p (g t)"))
@@ -225,6 +239,8 @@ def tile_invblock_pa_t_kernel(tc, u_old, v_old, W1, b1, out):
             transpose_rows(
                 nc, bank, [w_rows[n // PACK][:, n % PACK, :] for n in range(first, first + TILES_PER_BANK)], identity[:]
             )
+            if b % 2 == 0:
+                keep_tensor_clock_up(1)
             nc.scalar.copy(out=w1_pairs[:, first : first + TILES_PER_BANK], in_=words_side_by_side(bank[:]))
             units = slice(first * P, (first + TILES_PER_BANK) * P)
             quantise(

@@ -131,7 +131,7 @@ def tile_invblock_pa_t_kernel(tc, u_old, v_old, W1, b1, out):
         def live(c):
             return 0 <= c < N_CHUNKS
 
-        def transpose_u(c, second_copy):
+        def transpose_u(c, tiles_on_vector):
             grouped = stream.tile([P, CHUNK * PACK], BF16, name="u_grouped", align_bytes=64)
             pairs = grouped[:].bitcast(F32).rearrange("q (j r half) -> q j r half", j=ROW_TILES, half=HALVES)
             banks = []
@@ -140,8 +140,17 @@ def tile_invblock_pa_t_kernel(tc, u_old, v_old, W1, b1, out):
                 first = i * TILES_PER_BANK
                 transpose_rows(nc, bank, [u_rows[c][:, first + n, :] for n in range(TILES_PER_BANK)], identity[:])
                 banks.append(bank)
-            nc.scalar.copy(out=pairs[:, 0:TILES_PER_BANK], in_=words_side_by_side(banks[0][:]))
-            second_copy(out=pairs[:, TILES_PER_BANK:ROW_TILES], in_=words_side_by_side(banks[1][:]))
+            on_scalar = TILES_PER_BANK - tiles_on_vector
+            if tiles_on_vector:
+                nc.vector.tensor_copy(
+                    out=pairs[:, TILES_PER_BANK + on_scalar :], in_=words_side_by_side(banks[1][:, on_scalar:])
+                )
+            nc.scalar.copy(out=pairs[:, :TILES_PER_BANK], in_=words_side_by_side(banks[0][:]))
+            if on_scalar:
+                nc.scalar.copy(
+                    out=pairs[:, TILES_PER_BANK : TILES_PER_BANK + on_scalar],
+                    in_=words_side_by_side(banks[1][:, :on_scalar]),
+                )
             u_grouped[c] = grouped
 
         def quantise_u(c):
@@ -221,7 +230,7 @@ def tile_invblock_pa_t_kernel(tc, u_old, v_old, W1, b1, out):
             )
             nc.sync.dma_start(out=chunk_view(out, c)[:, j, cols], in_=out_rows[c][:, j, cols])
 
-        transpose_u(0, nc.vector.tensor_copy)
+        transpose_u(0, tiles_on_vector=2)
         keep_tensor_clock_up(1)
         quantise_u(0)
         bias = keep.tile([P, F_PASSES * PACK], F32)
@@ -262,13 +271,10 @@ def tile_invblock_pa_t_kernel(tc, u_old, v_old, W1, b1, out):
                 for g in range(F_PASSES):
                     group_four_rows_on_vector(nc, w2_grouped[:, g], w_rows[g][:])
             if live(c - 2):
-                finish_tile(c - 2, 0)
-                finish_tile(c - 2, 1)
+                for j in range(ROW_TILES):
+                    finish_tile(c - 2, j)
             if live(c + 1):
-                transpose_u(c + 1, nc.scalar.copy)
-            if live(c - 2):
-                finish_tile(c - 2, 2)
-                finish_tile(c - 2, 3)
+                transpose_u(c + 1, tiles_on_vector=1 if live(c - 2) else 0)
             if c == 1:
                 group_hidden(0, 1, group_four_rows_on_vector)
             if live(c - 1):

from contextlib import ExitStack

import concourse.mybir as mybir
from concourse.masks import make_identity

F32 = mybir.dt.float32
BF16 = mybir.dt.bfloat16
U32 = mybir.dt.uint32
U8 = mybir.dt.uint8
FP8X4 = mybir.dt.float8_e4m3fn_x4
TANH = mybir.ActivationFunctionType.Tanh
MULT = mybir.AluOpType.mult
ADD = mybir.AluOpType.add

B, HD, F = 4096, 512, 1024
STEP = 0.1
FLOPS = 2 * 2 * B * HD * F

P = 128
PACK = 4
K_PASS = P * PACK
CHUNK = 512
N_CHUNKS = B // CHUNK
ROW_TILES = CHUNK // P
F_PASSES = F // K_PASS
HALVES = 2
TILES_PER_BANK = 2
ALL_ROWS = slice(0, CHUNK)
ALL_COLS = slice(0, HD)
HEAD_WARMERS = 5
RUN = 4


def transpose_rows(nc, bank, row_tiles, identity):
    for i, rows in enumerate(row_tiles):
        words = rows.bitcast(F32)
        for half in range(HALVES):
            nc.tensor.transpose(bank[:, i, half, :], words[:, half * P : (half + 1) * P], identity)


def words_side_by_side(bank):
    return bank.rearrange("q i half r -> q i r half")


def group_four_rows_on_vector(nc, grouped, rows):
    nc.vector.tensor_copy(
        out=grouped.rearrange("p (c i) t -> p c t i", i=RUN),
        in_=rows.rearrange("p t (c i) -> p c t i", i=RUN),
    )


def group_four_rows_on_gpsimd(nc, grouped, rows):
    nc.gpsimd.tensor_scalar(
        out=grouped.rearrange("p (c i) t -> p c t i", i=RUN),
        in0=rows.rearrange("p t (c i) -> p c t i", i=RUN),
        scalar1=1.0,
        scalar2=0.0,
        op0=MULT,
        op1=ADD,
    )


def group_four_rows_on_scalar(nc, grouped, rows):
    nc.scalar.copy(
        out=grouped.rearrange("p (c i) t -> p c t i", i=RUN),
        in_=rows.rearrange("p t (c i) -> p c t i", i=RUN),
    )


def quantise(nc, codes, scales, grouped):
    nc.vector.quantize_mx(out=codes.bitcast(FP8X4), scales=scales, in_=grouped)


def tile_invblock_pa_t_kernel(tc, u_old, v_old, W1, b1, out):
    nc = tc.nc
    with ExitStack() as ctx:
        ctx.enter_context(tc.manual_schedule())
        keep = ctx.enter_context(tc.tile_pool(name="keep", bufs=1))
        stream = ctx.enter_context(tc.tile_pool(name="stream", bufs=2))
        psum = ctx.enter_context(tc.psum_pool(name="psum", bufs=4))

        def chunk_view(dram, c):
            return dram[c * CHUNK : (c + 1) * CHUNK, :].rearrange("(p j) h -> p j h", j=ROW_TILES)

        u_rows = [keep.tile([P, ROW_TILES, HD], BF16, name="u_rows%d" % c) for c in range(N_CHUNKS)]
        v_rows = [keep.tile([P, ROW_TILES, HD], BF16, name="v_rows%d" % c) for c in range(N_CHUNKS)]
        w_rows = [keep.tile([P, PACK, HD], BF16, name="w_rows%d" % g) for g in range(F_PASSES)]
        bias_bf16 = keep.tile([P, F_PASSES, PACK], BF16)

        nc.scalar.dma_start(out=bias_bf16[:], in_=b1.rearrange("(g p t) -> p g t", g=F_PASSES, t=PACK))
        for first in range(0, ROW_TILES, TILES_PER_BANK):
            tiles = slice(first, first + TILES_PER_BANK)
            nc.sync.dma_start(out=u_rows[0][:, tiles, :], in_=chunk_view(u_old, 0)[:, tiles, :])
        for g in range(F_PASSES):
            rows_of_pass = W1[g * K_PASS : (g + 1) * K_PASS, :].rearrange("(p t) k -> p t k", t=PACK)
            for first in range(0, PACK, TILES_PER_BANK):
                tiles = slice(first, first + TILES_PER_BANK)
                nc.sync.dma_start(out=w_rows[g][:, tiles, :], in_=rows_of_pass[:, tiles, :])
        for c in range(1, N_CHUNKS):
            nc.sync.dma_start(out=u_rows[c][:], in_=chunk_view(u_old, c))
            nc.sync.dma_start(out=v_rows[c - 1][:], in_=chunk_view(v_old, c - 1))
        nc.sync.dma_start(out=v_rows[N_CHUNKS - 1][:], in_=chunk_view(v_old, N_CHUNKS - 1))

        identity = keep.tile([P, P], F32)
        make_identity(nc, identity[:])
        idle_operand = keep.tile([P, CHUNK], BF16)
        nc.vector.memset(idle_operand[:], 0.0)
        zero_column = keep.tile([P, 1], F32)
        warm_column = keep.tile([P, 1], F32)
        nc.vector.memset(zero_column[:], 0.0)
        nc.scalar.activation(out=warm_column[:], in_=zero_column[:], func=TANH)

        idle_acc = psum.tile([P, CHUNK], F32, name="idle_acc", tag="shared")

        def keep_tensor_clock_up(count):
            for unused in range(count):
                nc.tensor.matmul(
                    idle_acc[:], lhsT=idle_operand[:, 0:P], rhs=idle_operand[:], start=True, stop=True
                )

        keep_tensor_clock_up(HEAD_WARMERS)

        u_grouped = {}
        u_quantised = {}
        hidden = {}
        hidden_grouped = {}
        hidden_quantised = {}
        out_acc = {}
        out_rows = {}

        def live(c):
            return 0 <= c < N_CHUNKS

        def transpose_u(c, tiles_on_vector):
            grouped = stream.tile([P, CHUNK * PACK], BF16, name="u_grouped", align_bytes=64)
            pairs = grouped[:].bitcast(F32).rearrange("q (j r half) -> q j r half", j=ROW_TILES, half=HALVES)
            banks = []
            for i in range(ROW_TILES // TILES_PER_BANK):
                bank = psum.tile([P, TILES_PER_BANK, HALVES, P], F32, name="u_bank", tag="shared")
                first = i * TILES_PER_BANK
                transpose_rows(nc, bank, [u_rows[c][:, first + n, :] for n in range(TILES_PER_BANK)], identity[:])
                banks.append(bank)
            on_scalar = TILES_PER_BANK - tiles_on_vector
            if tiles_on_vector:
                nc.vector.tensor_copy(
                    out=pairs[:, TILES_PER_BANK + on_scalar :], in_=words_side_by_side(banks[1][:, on_scalar:])
                )
            nc.scalar.copy(out=pairs[:, :TILES_PER_BANK], in_=words_side_by_side(banks[0][:]))
            if on_scalar:
                nc.scalar.copy(
                    out=pairs[:, TILES_PER_BANK : TILES_PER_BANK + on_scalar],
                    in_=words_side_by_side(banks[1][:, :on_scalar]),
                )
            u_grouped[c] = grouped

        def quantise_u(c):
            codes = stream.tile([P, CHUNK], U32, name="u_codes", align_bytes=64)
            scales = stream.tile([P, CHUNK], U8, name="u_scales", align_bytes=64)
            quantise(nc, codes[:], scales[:], u_grouped[c][:])
            u_quantised[c] = (codes, scales)

        def hidden_layer(c, g):
            u_codes, u_scales = u_quantised[c]
            hidden[(c, g)] = stream.tile([P, PACK, CHUNK], BF16, name="hidden", bufs=3)
            for t in range(PACK):
                column = g * PACK + t
                units = slice(column * P, (column + 1) * P)
                acc = psum.tile([P, CHUNK], F32, name="hidden_acc", tag="hidden_acc")
                nc.tensor.matmul_mx(
                    out=acc[:],
                    lhsT=w1_codes[:, units].bitcast(FP8X4),
                    lhsT_scale=w1_scales[:, units],
                    rhs=u_codes[:].bitcast(FP8X4),
                    rhs_scale=u_scales[:],
                    start=True,
                    stop=True,
                )
                nc.scalar.activation(
                    out=hidden[(c, g)][:, t, :], in_=acc[:], func=TANH, bias=bias[:, column : column + 1]
                )

        def group_hidden(c, g, group_four_rows, rows=ALL_ROWS):
            if (c, g) not in hidden_grouped:
                on_gpsimd = group_four_rows is group_four_rows_on_gpsimd
                hidden_grouped[(c, g)] = stream.tile(
                    [P, CHUNK, PACK],
                    BF16,
                    name="hidden_grouped",
                    tag="grouped_on_gpsimd" if on_gpsimd else "grouped",
                    bufs=1 if on_gpsimd else 2,
                    align_bytes=64,
                )
            group_four_rows(nc, hidden_grouped[(c, g)][:, rows, :], hidden[(c, g)][:, :, rows])

        def quantise_hidden(c, g, rows=ALL_ROWS):
            if c not in hidden_quantised:
                codes = stream.tile([P, F_PASSES, CHUNK], U32, name="hidden_codes", align_bytes=64)
                scales = stream.tile([P, F_PASSES, CHUNK], U8, name="hidden_scales", align_bytes=64)
                hidden_quantised[c] = (codes, scales)
            codes, scales = hidden_quantised[c]
            grouped = hidden_grouped[(c, g)][:, rows, :]
            quantise(nc, codes[:, g, rows], scales[:, g, rows], grouped.rearrange("p n t -> p (n t)"))

        def second_matmul(c, j, passes=range(F_PASSES)):
            codes, scales = hidden_quantised[c]
            rows = slice(j * P, (j + 1) * P)
            if (c, j) not in out_acc:
                out_acc[(c, j)] = psum.tile([P, HD], F32, name="out_acc", tag="shared")
            for g in passes:
                nc.tensor.matmul_mx(
                    out=out_acc[(c, j)][:],
                    lhsT=codes[:, g, rows].bitcast(FP8X4),
                    lhsT_scale=scales[:, g, rows],
                    rhs=w2_codes[:, g, :].bitcast(FP8X4),
                    rhs_scale=w2_scales[:, g, :],
                    start=(g == 0),
                    stop=(g == F_PASSES - 1),
                )

        def finish_tile(c, j, cols=ALL_COLS):
            if c not in out_rows:
                out_rows[c] = stream.tile([P, ROW_TILES, HD], F32, name="out_rows", bufs=3)
            nc.vector.scalar_tensor_tensor(
                out=out_rows[c][:, j, cols],
                in0=out_acc[(c, j)][:, cols],
                scalar=STEP,
                in1=v_rows[c][:, j, cols],
                op0=MULT,
                op1=ADD,
            )
            nc.sync.dma_start(out=chunk_view(out, c)[:, j, cols], in_=out_rows[c][:, j, cols])

        transpose_u(0, tiles_on_vector=2)
        keep_tensor_clock_up(1)
        quantise_u(0)
        bias = keep.tile([P, F_PASSES * PACK], F32)
        nc.vector.tensor_copy(out=bias[:], in_=bias_bf16[:].rearrange("p g t -> p (g t)"))

        w1_grouped = keep.tile([P, F * PACK], BF16, align_bytes=64)
        w1_codes = keep.tile([P, F], U32, align_bytes=64)
        w1_scales = keep.tile([P, F], U8, align_bytes=64)
        w1_pairs = w1_grouped[:].bitcast(F32).rearrange(
            "q (f r half) -> q f r half", f=F_PASSES * PACK, half=HALVES
        )
        for b in range(F_PASSES * PACK // TILES_PER_BANK):
            first = b * TILES_PER_BANK
            bank = psum.tile([P, TILES_PER_BANK, HALVES, P], F32, name="w_bank", tag="hidden_acc")
            transpose_rows(
                nc, bank, [w_rows[n // PACK][:, n % PACK, :] for n in range(first, first + TILES_PER_BANK)], identity[:]
            )
            if b % 2 == 0:
                keep_tensor_clock_up(1)
            nc.scalar.copy(out=w1_pairs[:, first : first + TILES_PER_BANK], in_=words_side_by_side(bank[:]))
            units = slice(first * P, (first + TILES_PER_BANK) * P)
            quantise(
                nc,
                w1_codes[:, units],
                w1_scales[:, units],
                w1_grouped[:, first * P * PACK : (first + TILES_PER_BANK) * P * PACK],
            )

        w2_grouped = keep.tile([P, F_PASSES, HD, PACK], BF16, align_bytes=64)
        w2_codes = keep.tile([P, F_PASSES, HD], U32, align_bytes=64)
        w2_scales = keep.tile([P, F_PASSES, HD], U8, align_bytes=64)

        hidden_layer(0, 0)
        for c in range(N_CHUNKS):
            if live(c - 2):
                group_hidden(c - 1, 1, group_four_rows_on_gpsimd)
            if c == 0:
                for g in range(F_PASSES):
                    group_four_rows_on_vector(nc, w2_grouped[:, g], w_rows[g][:])
            if live(c - 2):
                for j in range(ROW_TILES):
                    finish_tile(c - 2, j)
            if live(c + 1):
                transpose_u(c + 1, tiles_on_vector=1 if live(c - 2) else 0)
            if c == 1:
                group_hidden(0, 1, group_four_rows_on_vector)
            if live(c - 1):
                quantise_hidden(c - 1, 1)
            group_hidden(c, 0, group_four_rows_on_vector if live(c + 1) else group_four_rows_on_gpsimd)
            hidden_layer(c, 1)
            if live(c + 1):
                quantise_u(c + 1)
                quantise_hidden(c, 0)
            if c == 0:
                quantise(
                    nc,
                    w2_codes[:].rearrange("p g h -> p (g h)"),
                    w2_scales[:].rearrange("p g h -> p (g h)"),
                    w2_grouped[:].rearrange("p g h t -> p (g h t)"),
                )
            if live(c - 1):
                for j in range(ROW_TILES - 1):
                    second_matmul(c - 1, j)
            if live(c + 1):
                hidden_layer(c + 1, 0)
            if live(c - 1):
                second_matmul(c - 1, ROW_TILES - 1)

        last = N_CHUNKS - 1
        for j in range(ROW_TILES):
            finish_tile(last - 1, j)
        quantise_hidden(last, 0)
        halves = [slice(h * CHUNK // 2, (h + 1) * CHUNK // 2) for h in range(2)]
        tiles_per_half = ROW_TILES // 2
        for rows in halves:
            group_hidden(last, 1, group_four_rows_on_scalar, rows)
        for rows in halves:
            quantise_hidden(last, 1, rows)
        for first in range(0, ROW_TILES, tiles_per_half):
            for g in range(F_PASSES):
                for j in range(first, first + tiles_per_half):
                    second_matmul(last, j, passes=(g,))
        for j in range(ROW_TILES - 1):
            finish_tile(last, j)
        for h in range(2):
            finish_tile(last, ROW_TILES - 1, slice(h * HD // 2, (h + 1) * HD // 2))
